import numpy as np
import ml_dtypes

BF16 = ml_dtypes.bfloat16


def bf(x):
    return np.asarray(x, np.float32).astype(BF16)


def f32(x):
    return np.asarray(x, np.float32)


def f64(x):
    return np.asarray(x).astype(np.float64)


def striped(idx):
    return np.tile(idx.reshape(-1, 16).T, (8, 1))


E, S, N, H, K = 256, 4096, 4096, 128, 128
SPARSITY = 0.7
SLOPE = 0.01


def setup_inputs():
    vals = np.random.uniform(size=(1, N)) * 5.0
    drop = np.random.uniform(size=(1, N)) < SPARSITY
    return {"gene_embed": f32(0.5 * np.random.standard_normal((E, S))), "expr": f32(np.where(drop, 0.0, vals)), "w1": f32(0.5 * np.random.standard_normal((H, 1))), "b1": f32(0.1 * np.random.standard_normal((H, 1))), "w2": bf(np.random.standard_normal((H, K)) / np.sqrt(H)), "b2": f32(0.1 * np.random.standard_normal((K, 1))), "bin0": f32(0.5 * np.random.standard_normal((E, 1))), "bins": bf(4.0 * np.random.standard_normal((K, E))), "offs": striped(np.random.permutation(np.tile(np.arange(S), 2))[:N])}


def reference(gene_embed, expr, w1, b1, w2, b2, bin0, bins, offs):
    idx = offs[:16].T.reshape(-1)
    x = f64(expr)
    m = np.where(x != 0.0, 1.0, 0.0)
    v = f64(w1) * x + f64(b1)
    hid = np.maximum(v, SLOPE * v)
    logit = f64(w2).T @ hid + f64(b2)
    ex = np.exp(logit)
    p = ex / ex.sum(axis=0, keepdims=True)
    q = f64(bins).T @ p
    t = f64(gene_embed)[:, idx] + (1.0 - m) * f64(bin0)
    return t + m * q

@@ -1,0 +1,107 @@
+import concourse.mybir as mybir
+from concourse.masks import make_identity
+
+FP32 = mybir.dt.float32
+BF16 = mybir.dt.bfloat16
+U16 = mybir.dt.uint16
+ALU = mybir.AluOpType
+ACT = mybir.ActivationFunctionType
+
+P = 128
+E, S, N, H, K = 256, 4096, 4096, 128, 128
+SLOPE = 0.01
+E_BLOCKS = E // P
+PIECE = 512
+PIECES = N // PIECE
+GROUPS = PIECE // P
+LOAD = 1024
+
+FLOPS = 2 * N * (H * K + K * E)
+
+
+def tile_tokenizer_kernel(tc, gene_embed, expr, w1, b1, w2, b2, bin0, bins, offs, out):
+    nc = tc.nc
+    with (
+        tc.tile_pool(name="held", bufs=1) as held,
+        tc.psum_pool(name="psum", bufs=2) as psum,
+    ):
+        offsets = held.tile([P, N // 16], U16, name="offsets")
+        nc.sync.dma_start(offsets[:], offs)
+        x_all = held.tile([P, N], FP32, name="x_all")
+        for c in range(0, N, LOAD):
+            nc.sync.dma_start(x_all[:, c : c + LOAD], expr[0:1, c : c + LOAD].broadcast_to([P, LOAD]))
+        window = [held.tile([P, S], FP32, name=f"window{eb}") for eb in range(E_BLOCKS)]
+        for eb in range(E_BLOCKS):
+            nc.sync.dma_start(window[eb][:], gene_embed[eb * P : (eb + 1) * P, :])
+
+        w1_sb = held.tile([P, 1], FP32, name="w1_sb")
+        b1_sb = held.tile([P, 1], FP32, name="b1_sb")
+        b2_sb = held.tile([P, 1], FP32, name="b2_sb")
+        w2_sb = held.tile([H, K], BF16, name="w2_sb")
+        bins_sb = held.tile([K, E], BF16, name="bins_sb")
+        for tile, source in ((w1_sb, w1), (b1_sb, b1), (w2_sb, w2), (b2_sb, b2), (bins_sb, bins)):
+            nc.scalar.dma_start(tile[:], source)
+        bin0_sb = [held.tile([P, 1], FP32, name=f"bin0_sb{eb}") for eb in range(E_BLOCKS)]
+        for eb in range(E_BLOCKS):
+            nc.gpsimd.dma_start(bin0_sb[eb][:], bin0[eb * P : (eb + 1) * P, :])
+        x_col = held.tile([P, N // P], FP32, name="x_col")
+        with nc.allow_non_contiguous_dma(reason="16 KiB, one token to a partition"):
+            nc.gpsimd.dma_start(x_col[:], expr.rearrange("o (g r) -> r (o g)", r=P))
+
+        identity = held.tile([P, P], FP32, name="identity")
+        make_identity(nc, identity[:])
+        ones = held.tile([K, 1], BF16, name="ones")
+        nc.vector.memset(ones[:], 1.0)
+        w1_neg = held.tile([P, 1], FP32, name="w1_neg")
+        b1_neg = held.tile([P, 1], FP32, name="b1_neg")
+        w2_neg = held.tile([H, K], BF16, name="w2_neg")
+        nc.vector.tensor_scalar_mul(w1_neg[:], w1_sb[:], -SLOPE)
+        nc.vector.tensor_scalar_mul(b1_neg[:], b1_sb[:], -SLOPE)
+        nc.vector.tensor_scalar_mul(w2_neg[:], w2_sb[:], -1.0)
+        m_col = held.tile([P, N // P], FP32, name="m_col")
+        nc.vector.tensor_single_scalar(m_col[:], x_col[:], 0.0, ALU.not_equal)
+
+        zero_bin = [held.tile([P, N], FP32, name=f"zero_bin{eb}") for eb in range(E_BLOCKS)]
+        hid_pos = held.tile([H, N], BF16, name="hid_pos")
+        hid_neg = held.tile([H, N], BF16, name="hid_neg")
+        expo = held.tile([K, N], BF16, name="expo")
+        inv_col = held.tile([P, N // P], FP32, name="inv_col")
+        scale_col = held.tile([P, N // P], FP32, name="scale_col")
+        prob = held.tile([K, N], BF16, name="prob")
+        t = [held.tile([P, N], FP32, name=f"t{eb}") for eb in range(E_BLOCKS)]
+        result = [held.tile([P, N], FP32, name=f"result{eb}") for eb in range(E_BLOCKS)]
+
+        for i in range(PIECES):
+            cols = slice(i * PIECE, (i + 1) * PIECE)
+            groups = slice(i * GROUPS, (i + 1) * GROUPS)
+            for eb in range(E_BLOCKS):
+                nc.vector.tensor_scalar(
+                    zero_bin[eb][:, cols], x_all[:, cols], 0.0, bin0_sb[eb][:], ALU.is_equal, ALU.mult
+                )
+            nc.scalar.activation(hid_pos[:, cols], x_all[:, cols], ACT.Relu, bias=b1_sb[:], scale=w1_sb[:])
+            nc.scalar.activation(hid_neg[:, cols], x_all[:, cols], ACT.Relu, bias=b1_neg[:], scale=w1_neg[:])
+            logit = psum.tile([K, PIECE], FP32, name="logit")
+            nc.tensor.matmul(logit[:], w2_sb[:], hid_pos[:, cols], start=True, stop=False)
+            nc.tensor.matmul(logit[:], w2_neg[:], hid_neg[:, cols], start=False, stop=True)
+            nc.scalar.activation(expo[:, cols], logit[:], ACT.Exp, bias=b2_sb[:], scale=1.0)
+            sum_col = psum.tile([P, GROUPS], FP32, name="sum_col")
+            for g in range(GROUPS):
+                tokens = slice(i * PIECE + g * P, i * PIECE + (g + 1) * P)
+                nc.tensor.matmul(sum_col[:, g : g + 1], expo[:, tokens], ones[:], start=True, stop=True)
+            nc.vector.reciprocal(inv_col[:, groups], sum_col[:])
+            nc.vector.tensor_tensor(scale_col[:, groups], inv_col[:, groups], m_col[:, groups], ALU.mult)
+            scale_all = psum.tile([K, PIECE], FP32, name="scale_all")
+            for g in range(GROUPS):
+                column = scale_col[:, i * GROUPS + g : i * GROUPS + g + 1]
+                nc.tensor.transpose(scale_all[:, g * P : (g + 1) * P], column.to_broadcast([P, K]), identity[:])
+            nc.vector.tensor_tensor(prob[:, cols], expo[:, cols], scale_all[:], ALU.mult)
+
+        for eb in range(E_BLOCKS):
+            for i in range(PIECES):
+                cols = slice(i * PIECE, (i + 1) * PIECE)
+                picked = window[eb][:].indirect(offsets[:, i * (PIECE // 16) : (i + 1) * (PIECE // 16)])
+                nc.vector.tensor_tensor(t[eb][:, cols], picked, zero_bin[eb][:, cols], ALU.add)
+                mixed = psum.tile([P, PIECE], FP32, name="mixed")
+                nc.tensor.matmul(mixed[:], bins_sb[:, eb * P : (eb + 1) * P], prob[:, cols], start=True, stop=True)
+                nc.vector.tensor_tensor(result[eb][:, cols], t[eb][:, cols], mixed[:], ALU.add)
+                nc.sync.dma_start(out[eb * P : (eb + 1) * P, cols], result[eb][:, cols])

@@ -1,3 +1,5 @@
+from contextlib import ExitStack
+
 import concourse.mybir as mybir
 from concourse.masks import make_identity
 
@@ -21,10 +23,8 @@ FLOPS = 2 * N * (H * K + K * E)
 
 def tile_tokenizer_kernel(tc, gene_embed, expr, w1, b1, w2, b2, bin0, bins, offs, out):
     nc = tc.nc
-    with (
-        tc.tile_pool(name="held", bufs=1) as held,
-        tc.psum_pool(name="psum", bufs=2) as psum,
-    ):
+    with ExitStack() as ctx:
+        held = ctx.enter_context(tc.tile_pool(name="held", bufs=1))
         offsets = held.tile([P, N // 16], U16, name="offsets")
         nc.sync.dma_start(offsets[:], offs)
         x_all = held.tile([P, N], FP32, name="x_all")
@@ -44,9 +44,9 @@ def tile_tokenizer_kernel(tc, gene_embed, expr, w1, b1, w2, b2, bin0, bins, offs
         bin0_sb = [held.tile([P, 1], FP32, name=f"bin0_sb{eb}") for eb in range(E_BLOCKS)]
         for eb in range(E_BLOCKS):
             nc.gpsimd.dma_start(bin0_sb[eb][:], bin0[eb * P : (eb + 1) * P, :])
-        x_col = held.tile([P, N // P], FP32, name="x_col")
-        with nc.allow_non_contiguous_dma(reason="16 KiB, one token to a partition"):
-            nc.gpsimd.dma_start(x_col[:], expr.rearrange("o (g r) -> r (o g)", r=P))
+        x_rows = held.tile([P, P], FP32, name="x_rows")
+        nc.gpsimd.memset(x_rows[:], 0.0)
+        nc.gpsimd.dma_start(x_rows[0 : N // P, :], expr.rearrange("o (g r) -> (o g) r", r=P))
 
         identity = held.tile([P, P], FP32, name="identity")
         make_identity(nc, identity[:])
@@ -59,7 +59,10 @@ def tile_tokenizer_kernel(tc, gene_embed, expr, w1, b1, w2, b2, bin0, bins, offs
         nc.vector.tensor_scalar_mul(b1_neg[:], b1_sb[:], -SLOPE)
         nc.vector.tensor_scalar_mul(w2_neg[:], w2_sb[:], -1.0)
         m_col = held.tile([P, N // P], FP32, name="m_col")
-        nc.vector.tensor_single_scalar(m_col[:], x_col[:], 0.0, ALU.not_equal)
+        with tc.psum_pool(name="psum_once", bufs=1) as psum_once:
+            x_col = psum_once.tile([P, P], FP32, name="x_col")
+            nc.tensor.transpose(x_col[:], x_rows[:], identity[:])
+            nc.vector.tensor_single_scalar(m_col[:], x_col[:, 0 : N // P], 0.0, ALU.not_equal)
 
         zero_bin = [held.tile([P, N], FP32, name=f"zero_bin{eb}") for eb in range(E_BLOCKS)]
         hid_pos = held.tile([H, N], BF16, name="hid_pos")
@@ -70,6 +73,8 @@ def tile_tokenizer_kernel(tc, gene_embed, expr, w1, b1, w2, b2, bin0, bins, offs
         prob = held.tile([K, N], BF16, name="prob")
         t = [held.tile([P, N], FP32, name=f"t{eb}") for eb in range(E_BLOCKS)]
         result = [held.tile([P, N], FP32, name=f"result{eb}") for eb in range(E_BLOCKS)]
+
+        psum = ctx.enter_context(tc.psum_pool(name="psum", bufs=2))
 
         for i in range(PIECES):
             cols = slice(i * PIECE, (i + 1) * PIECE)

@@ -16,7 +16,10 @@ E_BLOCKS = E // P
 PIECE = 512
 PIECES = N // PIECE
 GROUPS = PIECE // P
+BANK_GROUPS = PIECE // E
 LOAD = 1024
+AHEAD = 2
+LAG = 3
 
 FLOPS = 2 * N * (H * K + K * E)
 
@@ -27,26 +30,26 @@ def tile_tokenizer_kernel(tc, gene_embed, expr, w1, b1, w2, b2, bin0, bins, offs
         held = ctx.enter_context(tc.tile_pool(name="held", bufs=1))
         offsets = held.tile([P, N // 16], U16, name="offsets")
         nc.sync.dma_start(offsets[:], offs)
-        x_all = held.tile([P, N], FP32, name="x_all")
-        for c in range(0, N, LOAD):
-            nc.sync.dma_start(x_all[:, c : c + LOAD], expr[0:1, c : c + LOAD].broadcast_to([P, LOAD]))
-        window = [held.tile([P, S], FP32, name=f"window{eb}") for eb in range(E_BLOCKS)]
-        for eb in range(E_BLOCKS):
-            nc.sync.dma_start(window[eb][:], gene_embed[eb * P : (eb + 1) * P, :])
-
         w1_sb = held.tile([P, 1], FP32, name="w1_sb")
         b1_sb = held.tile([P, 1], FP32, name="b1_sb")
         b2_sb = held.tile([P, 1], FP32, name="b2_sb")
         w2_sb = held.tile([H, K], BF16, name="w2_sb")
         bins_sb = held.tile([K, E], BF16, name="bins_sb")
         for tile, source in ((w1_sb, w1), (b1_sb, b1), (w2_sb, w2), (b2_sb, b2), (bins_sb, bins)):
-            nc.scalar.dma_start(tile[:], source)
+            nc.sync.dma_start(tile[:], source)
         bin0_sb = [held.tile([P, 1], FP32, name=f"bin0_sb{eb}") for eb in range(E_BLOCKS)]
         for eb in range(E_BLOCKS):
-            nc.gpsimd.dma_start(bin0_sb[eb][:], bin0[eb * P : (eb + 1) * P, :])
+            nc.sync.dma_start(bin0_sb[eb][:], bin0[eb * P : (eb + 1) * P, :])
         x_rows = held.tile([P, P], FP32, name="x_rows")
-        nc.gpsimd.memset(x_rows[:], 0.0)
-        nc.gpsimd.dma_start(x_rows[0 : N // P, :], expr.rearrange("o (g r) -> (o g) r", r=P))
+        nc.vector.memset(x_rows[:], 0.0)
+        nc.sync.dma_start(x_rows[0 : N // P, :], expr.rearrange("o (g r) -> (o g) r", r=P))
+        x_all = held.tile([P, N], FP32, name="x_all")
+        window = [held.tile([P, S], FP32, name=f"window{eb}") for eb in range(E_BLOCKS)]
+        for c in range(N // LOAD):
+            tokens = slice(c * LOAD, (c + 1) * LOAD)
+            nc.sync.dma_start(x_all[:, tokens], expr[0:1, tokens].broadcast_to([P, LOAD]))
+            if c < E_BLOCKS:
+                nc.sync.dma_start(window[c][:], gene_embed[c * P : (c + 1) * P, :])
 
         identity = held.tile([P, P], FP32, name="identity")
         make_identity(nc, identity[:])
@@ -70,13 +73,13 @@ def tile_tokenizer_kernel(tc, gene_embed, expr, w1, b1, w2, b2, bin0, bins, offs
         expo = held.tile([K, N], BF16, name="expo")
         inv_col = held.tile([P, N // P], FP32, name="inv_col")
         scale_col = held.tile([P, N // P], FP32, name="scale_col")
-        prob = held.tile([K, N], BF16, name="prob")
-        t = [held.tile([P, N], FP32, name=f"t{eb}") for eb in range(E_BLOCKS)]
+        q_tok = held.tile([P, N // P, E], FP32, name="q_tok")
         result = [held.tile([P, N], FP32, name=f"result{eb}") for eb in range(E_BLOCKS)]
 
+        ring = ctx.enter_context(tc.tile_pool(name="ring", bufs=3))
         psum = ctx.enter_context(tc.psum_pool(name="psum", bufs=2))
 
-        for i in range(PIECES):
+        def mixture(i):
             cols = slice(i * PIECE, (i + 1) * PIECE)
             groups = slice(i * GROUPS, (i + 1) * GROUPS)
             for eb in range(E_BLOCKS):
@@ -90,23 +93,36 @@ def tile_tokenizer_kernel(tc, gene_embed, expr, w1, b1, w2, b2, bin0, bins, offs
             nc.tensor.matmul(logit[:], w2_neg[:], hid_neg[:, cols], start=False, stop=True)
             nc.scalar.activation(expo[:, cols], logit[:], ACT.Exp, bias=b2_sb[:], scale=1.0)
             sum_col = psum.tile([P, GROUPS], FP32, name="sum_col")
-            for g in range(GROUPS):
-                tokens = slice(i * PIECE + g * P, i * PIECE + (g + 1) * P)
-                nc.tensor.matmul(sum_col[:, g : g + 1], expo[:, tokens], ones[:], start=True, stop=True)
+            for a in range(GROUPS):
+                g = i * GROUPS + a
+                nc.tensor.matmul(sum_col[:, a : a + 1], expo[:, g * P : (g + 1) * P], ones[:], start=True, stop=True)
             nc.vector.reciprocal(inv_col[:, groups], sum_col[:])
             nc.vector.tensor_tensor(scale_col[:, groups], inv_col[:, groups], m_col[:, groups], ALU.mult)
-            scale_all = psum.tile([K, PIECE], FP32, name="scale_all")
-            for g in range(GROUPS):
-                column = scale_col[:, i * GROUPS + g : i * GROUPS + g + 1]
-                nc.tensor.transpose(scale_all[:, g * P : (g + 1) * P], column.to_broadcast([P, K]), identity[:])
-            nc.vector.tensor_tensor(prob[:, cols], expo[:, cols], scale_all[:], ALU.mult)
+            for first in range(0, GROUPS, BANK_GROUPS):
+                mix_tok = psum.tile([P, BANK_GROUPS, E], FP32, name="mix_tok")
+                for a in range(BANK_GROUPS):
+                    g = i * GROUPS + first + a
+                    nc.tensor.matmul(mix_tok[:, a, :], expo[:, g * P : (g + 1) * P], bins_sb[:], start=True, stop=True)
+                for a in range(BANK_GROUPS):
+                    g = i * GROUPS + first + a
+                    nc.scalar.activation(q_tok[:, g, :], mix_tok[:, a, :], ACT.Copy, scale=scale_col[:, g : g + 1])
 
-        for eb in range(E_BLOCKS):
-            for i in range(PIECES):
-                cols = slice(i * PIECE, (i + 1) * PIECE)
-                picked = window[eb][:].indirect(offsets[:, i * (PIECE // 16) : (i + 1) * (PIECE // 16)])
-                nc.vector.tensor_tensor(t[eb][:, cols], picked, zero_bin[eb][:, cols], ALU.add)
-                mixed = psum.tile([P, PIECE], FP32, name="mixed")
-                nc.tensor.matmul(mixed[:], bins_sb[:, eb * P : (eb + 1) * P], prob[:, cols], start=True, stop=True)
-                nc.vector.tensor_tensor(result[eb][:, cols], t[eb][:, cols], mixed[:], ALU.add)
-                nc.sync.dma_start(out[eb * P : (eb + 1) * P, cols], result[eb][:, cols])
+        def look_up(eb, i):
+            cols = slice(i * PIECE, (i + 1) * PIECE)
+            picked = window[eb][:].indirect(offsets[:, i * (PIECE // 16) : (i + 1) * (PIECE // 16)])
+            t = ring.tile([P, PIECE], FP32, name="t")
+            nc.vector.tensor_tensor(t[:], picked, zero_bin[eb][:, cols], ALU.add)
+            mixed = psum.tile([P, PIECE], FP32, name="mixed")
+            for a in range(GROUPS):
+                g = i * GROUPS + a
+                nc.tensor.transpose(mixed[:, a * P : (a + 1) * P], q_tok[:, g, eb * P : (eb + 1) * P], identity[:])
+            nc.vector.tensor_tensor(result[eb][:, cols], t[:], mixed[:], ALU.add)
+            nc.sync.dma_start(out[eb * P : (eb + 1) * P, cols], result[eb][:, cols])
+
+        for step in range(-AHEAD, PIECES + LAG):
+            if step + AHEAD < PIECES:
+                mixture(step + AHEAD)
+            if 0 <= step - LAG:
+                look_up(1, step - LAG)
+            if 0 <= step < PIECES:
+                look_up(0, step)

@@ -35,11 +35,12 @@ def tile_tokenizer_kernel(tc, gene_embed, expr, w1, b1, w2, b2, bin0, bins, offs
         b2_sb = held.tile([P, 1], FP32, name="b2_sb")
         w2_sb = held.tile([H, K], BF16, name="w2_sb")
         bins_sb = held.tile([K, E], BF16, name="bins_sb")
-        for tile, source in ((w1_sb, w1), (b1_sb, b1), (w2_sb, w2), (b2_sb, b2), (bins_sb, bins)):
+        for tile, source in ((w1_sb, w1), (b1_sb, b1)):
             nc.sync.dma_start(tile[:], source)
-        bin0_sb = [held.tile([P, 1], FP32, name=f"bin0_sb{eb}") for eb in range(E_BLOCKS)]
-        for eb in range(E_BLOCKS):
-            nc.sync.dma_start(bin0_sb[eb][:], bin0[eb * P : (eb + 1) * P, :])
+        for tile, source in ((w2_sb, w2), (b2_sb, b2), (bins_sb, bins)):
+            nc.scalar.dma_start(tile[:], source)
+        bin0_sb = held.tile([P, E_BLOCKS], FP32, name="bin0_sb")
+        nc.sync.dma_start(bin0_sb[:], bin0.rearrange("(eb p) o -> p (eb o)", p=P))
         x_rows = held.tile([P, P], FP32, name="x_rows")
         nc.vector.memset(x_rows[:], 0.0)
         nc.sync.dma_start(x_rows[0 : N // P, :], expr.rearrange("o (g r) -> (o g) r", r=P))
@@ -84,7 +85,7 @@ def tile_tokenizer_kernel(tc, gene_embed, expr, w1, b1, w2, b2, bin0, bins, offs
             groups = slice(i * GROUPS, (i + 1) * GROUPS)
             for eb in range(E_BLOCKS):
                 nc.vector.tensor_scalar(
-                    zero_bin[eb][:, cols], x_all[:, cols], 0.0, bin0_sb[eb][:], ALU.is_equal, ALU.mult
+                    zero_bin[eb][:, cols], x_all[:, cols], 0.0, bin0_sb[:, eb : eb + 1], ALU.is_equal, ALU.mult
                 )
             nc.scalar.activation(hid_pos[:, cols], x_all[:, cols], ACT.Relu, bias=b1_sb[:], scale=w1_sb[:])
             nc.scalar.activation(hid_neg[:, cols], x_all[:, cols], ACT.Relu, bias=b1_neg[:], scale=w1_neg[:])

@@ -18,8 +18,7 @@ PIECES = N // PIECE
 GROUPS = PIECE // P
 BANK_GROUPS = PIECE // E
 LOAD = 1024
-AHEAD = 2
-LAG = 3
+PSUM_BANKS = 8
 
 FLOPS = 2 * N * (H * K + K * E)
 
@@ -28,6 +27,7 @@ def tile_tokenizer_kernel(tc, gene_embed, expr, w1, b1, w2, b2, bin0, bins, offs
     nc = tc.nc
     with ExitStack() as ctx:
         held = ctx.enter_context(tc.tile_pool(name="held", bufs=1))
+        shared = ctx.enter_context(tc.tile_pool(name="shared", bufs=1))
         offsets = held.tile([P, N // 16], U16, name="offsets")
         nc.sync.dma_start(offsets[:], offs)
         w1_sb = held.tile([P, 1], FP32, name="w1_sb")
@@ -35,22 +35,19 @@ def tile_tokenizer_kernel(tc, gene_embed, expr, w1, b1, w2, b2, bin0, bins, offs
         b2_sb = held.tile([P, 1], FP32, name="b2_sb")
         w2_sb = held.tile([H, K], BF16, name="w2_sb")
         bins_sb = held.tile([K, E], BF16, name="bins_sb")
-        for tile, source in ((w1_sb, w1), (b1_sb, b1)):
+        for tile, source in ((w1_sb, w1), (b1_sb, b1), (w2_sb, w2), (b2_sb, b2), (bins_sb, bins)):
             nc.sync.dma_start(tile[:], source)
-        for tile, source in ((w2_sb, w2), (b2_sb, b2), (bins_sb, bins)):
-            nc.scalar.dma_start(tile[:], source)
         bin0_sb = held.tile([P, E_BLOCKS], FP32, name="bin0_sb")
         nc.sync.dma_start(bin0_sb[:], bin0.rearrange("(eb p) o -> p (eb o)", p=P))
         x_rows = held.tile([P, P], FP32, name="x_rows")
         nc.vector.memset(x_rows[:], 0.0)
         nc.sync.dma_start(x_rows[0 : N // P, :], expr.rearrange("o (g r) -> (o g) r", r=P))
-        x_all = held.tile([P, N], FP32, name="x_all")
-        window = [held.tile([P, S], FP32, name=f"window{eb}") for eb in range(E_BLOCKS)]
+        x_all = shared.tile([P, N], FP32, name="x_all", tag="expr_then_window")
         for c in range(N // LOAD):
             tokens = slice(c * LOAD, (c + 1) * LOAD)
             nc.sync.dma_start(x_all[:, tokens], expr[0:1, tokens].broadcast_to([P, LOAD]))
-            if c < E_BLOCKS:
-                nc.sync.dma_start(window[c][:], gene_embed[c * P : (c + 1) * P, :])
+        window0 = held.tile([P, S], FP32, name="window0")
+        nc.sync.dma_start(window0[:], gene_embed[0:P, :])
 
         identity = held.tile([P, P], FP32, name="identity")
         make_identity(nc, identity[:])
@@ -62,68 +59,68 @@ def tile_tokenizer_kernel(tc, gene_embed, expr, w1, b1, w2, b2, bin0, bins, offs
         nc.vector.tensor_scalar_mul(w1_neg[:], w1_sb[:], -SLOPE)
         nc.vector.tensor_scalar_mul(b1_neg[:], b1_sb[:], -SLOPE)
         nc.vector.tensor_scalar_mul(w2_neg[:], w2_sb[:], -1.0)
-        m_col = held.tile([P, N // P], FP32, name="m_col")
-        with tc.psum_pool(name="psum_once", bufs=1) as psum_once:
-            x_col = psum_once.tile([P, P], FP32, name="x_col")
-            nc.tensor.transpose(x_col[:], x_rows[:], identity[:])
-            nc.vector.tensor_single_scalar(m_col[:], x_col[:, 0 : N // P], 0.0, ALU.not_equal)
 
         zero_bin = [held.tile([P, N], FP32, name=f"zero_bin{eb}") for eb in range(E_BLOCKS)]
+        t_all = [held.tile([P, N], FP32, name=f"t_all{eb}") for eb in range(E_BLOCKS)]
         hid_pos = held.tile([H, N], BF16, name="hid_pos")
         hid_neg = held.tile([H, N], BF16, name="hid_neg")
         expo = held.tile([K, N], BF16, name="expo")
+        m_col = held.tile([P, N // P], FP32, name="m_col")
         inv_col = held.tile([P, N // P], FP32, name="inv_col")
         scale_col = held.tile([P, N // P], FP32, name="scale_col")
         q_tok = held.tile([P, N // P, E], FP32, name="q_tok")
         result = [held.tile([P, N], FP32, name=f"result{eb}") for eb in range(E_BLOCKS)]
 
-        ring = ctx.enter_context(tc.tile_pool(name="ring", bufs=3))
-        psum = ctx.enter_context(tc.psum_pool(name="psum", bufs=2))
+        def look_up(eb, window):
+            nc.vector.tensor_tensor(t_all[eb][:], window[:].indirect(offsets[:]), zero_bin[eb][:], ALU.add)
 
-        def mixture(i):
-            cols = slice(i * PIECE, (i + 1) * PIECE)
-            groups = slice(i * GROUPS, (i + 1) * GROUPS)
+        for c in range(N // LOAD):
+            tokens = slice(c * LOAD, (c + 1) * LOAD)
             for eb in range(E_BLOCKS):
                 nc.vector.tensor_scalar(
-                    zero_bin[eb][:, cols], x_all[:, cols], 0.0, bin0_sb[:, eb : eb + 1], ALU.is_equal, ALU.mult
+                    zero_bin[eb][:, tokens], x_all[:, tokens], 0.0, bin0_sb[:, eb : eb + 1], ALU.is_equal, ALU.mult
                 )
+        for i in range(PIECES):
+            cols = slice(i * PIECE, (i + 1) * PIECE)
             nc.scalar.activation(hid_pos[:, cols], x_all[:, cols], ACT.Relu, bias=b1_sb[:], scale=w1_sb[:])
             nc.scalar.activation(hid_neg[:, cols], x_all[:, cols], ACT.Relu, bias=b1_neg[:], scale=w1_neg[:])
-            logit = psum.tile([K, PIECE], FP32, name="logit")
-            nc.tensor.matmul(logit[:], w2_sb[:], hid_pos[:, cols], start=True, stop=False)
-            nc.tensor.matmul(logit[:], w2_neg[:], hid_neg[:, cols], start=False, stop=True)
-            nc.scalar.activation(expo[:, cols], logit[:], ACT.Exp, bias=b2_sb[:], scale=1.0)
-            sum_col = psum.tile([P, GROUPS], FP32, name="sum_col")
-            for a in range(GROUPS):
-                g = i * GROUPS + a
-                nc.tensor.matmul(sum_col[:, a : a + 1], expo[:, g * P : (g + 1) * P], ones[:], start=True, stop=True)
-            nc.vector.reciprocal(inv_col[:, groups], sum_col[:])
-            nc.vector.tensor_tensor(scale_col[:, groups], inv_col[:, groups], m_col[:, groups], ALU.mult)
-            for first in range(0, GROUPS, BANK_GROUPS):
-                mix_tok = psum.tile([P, BANK_GROUPS, E], FP32, name="mix_tok")
-                for a in range(BANK_GROUPS):
-                    g = i * GROUPS + first + a
-                    nc.tensor.matmul(mix_tok[:, a, :], expo[:, g * P : (g + 1) * P], bins_sb[:], start=True, stop=True)
-                for a in range(BANK_GROUPS):
-                    g = i * GROUPS + first + a
-                    nc.scalar.activation(q_tok[:, g, :], mix_tok[:, a, :], ACT.Copy, scale=scale_col[:, g : g + 1])
+        window1 = shared.tile([P, S], FP32, name="window1", tag="expr_then_window")
+        nc.sync.dma_start(window1[:], gene_embed[P : 2 * P, :])
 
-        def look_up(eb, i):
+        look_up(0, window0)
+        with tc.psum_pool(name="psum_logit", bufs=4) as psum_logit, tc.psum_pool(name="psum_cols", bufs=1) as psum_cols:
+            x_col = psum_cols.tile([P, P], FP32, name="x_col")
+            nc.tensor.transpose(x_col[:], x_rows[:], identity[:])
+            nc.vector.tensor_single_scalar(m_col[:], x_col[:, 0 : N // P], 0.0, ALU.not_equal)
+            sum_col = psum_cols.tile([P, N // P], FP32, name="sum_col")
+            for i in range(PIECES):
+                cols = slice(i * PIECE, (i + 1) * PIECE)
+                logit = psum_logit.tile([K, PIECE], FP32, name="logit")
+                nc.tensor.matmul(logit[:], w2_sb[:], hid_pos[:, cols], start=True, stop=False)
+                nc.tensor.matmul(logit[:], w2_neg[:], hid_neg[:, cols], start=False, stop=True)
+                nc.scalar.activation(expo[:, cols], logit[:], ACT.Exp, bias=b2_sb[:], scale=1.0)
+                for g in range(i * GROUPS, (i + 1) * GROUPS):
+                    nc.tensor.matmul(sum_col[:, g : g + 1], expo[:, g * P : (g + 1) * P], ones[:], start=True, stop=True)
+            nc.vector.reciprocal(inv_col[:], sum_col[:])
+            nc.vector.tensor_tensor(scale_col[:], inv_col[:], m_col[:], ALU.mult)
+
+        look_up(1, window1)
+        psum_late = ctx.enter_context(tc.psum_pool(name="psum_late", bufs=PSUM_BANKS))
+        for first in range(0, N // P, BANK_GROUPS):
+            mix_tok = psum_late.tile([P, BANK_GROUPS, E], FP32, name="mix_tok", tag="bank")
+            for a in range(BANK_GROUPS):
+                g = first + a
+                nc.tensor.matmul(mix_tok[:, a, :], expo[:, g * P : (g + 1) * P], bins_sb[:], start=True, stop=True)
+            for a in range(BANK_GROUPS):
+                g = first + a
+                nc.scalar.activation(q_tok[:, g, :], mix_tok[:, a, :], ACT.Copy, scale=scale_col[:, g : g + 1])
+
+        for i in range(PIECES):
             cols = slice(i * PIECE, (i + 1) * PIECE)
-            picked = window[eb][:].indirect(offsets[:, i * (PIECE // 16) : (i + 1) * (PIECE // 16)])
-            t = ring.tile([P, PIECE], FP32, name="t")
-            nc.vector.tensor_tensor(t[:], picked, zero_bin[eb][:, cols], ALU.add)
-            mixed = psum.tile([P, PIECE], FP32, name="mixed")
-            for a in range(GROUPS):
-                g = i * GROUPS + a
-                nc.tensor.transpose(mixed[:, a * P : (a + 1) * P], q_tok[:, g, eb * P : (eb + 1) * P], identity[:])
-            nc.vector.tensor_tensor(result[eb][:, cols], t[:], mixed[:], ALU.add)
-            nc.sync.dma_start(out[eb * P : (eb + 1) * P, cols], result[eb][:, cols])
-
-        for step in range(-AHEAD, PIECES + LAG):
-            if step + AHEAD < PIECES:
-                mixture(step + AHEAD)
-            if 0 <= step - LAG:
-                look_up(1, step - LAG)
-            if 0 <= step < PIECES:
-                look_up(0, step)
+            for eb in range(E_BLOCKS):
+                mixed = psum_late.tile([P, PIECE], FP32, name="mixed", tag="bank")
+                for a in range(GROUPS):
+                    g = i * GROUPS + a
+                    nc.tensor.transpose(mixed[:, a * P : (a + 1) * P], q_tok[:, g, eb * P : (eb + 1) * P], identity[:])
+                nc.vector.tensor_tensor(result[eb][:, cols], t_all[eb][:, cols], mixed[:], ALU.add)
+                nc.sync.dma_start(out[eb * P : (eb + 1) * P, cols], result[eb][:, cols])

@@ -35,7 +35,7 @@ def tile_tokenizer_kernel(tc, gene_embed, expr, w1, b1, w2, b2, bin0, bins, offs
         b2_sb = held.tile([P, 1], FP32, name="b2_sb")
         w2_sb = held.tile([H, K], BF16, name="w2_sb")
         bins_sb = held.tile([K, E], BF16, name="bins_sb")
-        for tile, source in ((w1_sb, w1), (b1_sb, b1), (w2_sb, w2), (b2_sb, b2), (bins_sb, bins)):
+        for tile, source in ((w1_sb, w1), (b1_sb, b1), (w2_sb, w2)):
             nc.sync.dma_start(tile[:], source)
         bin0_sb = held.tile([P, E_BLOCKS], FP32, name="bin0_sb")
         nc.sync.dma_start(bin0_sb[:], bin0.rearrange("(eb p) o -> p (eb o)", p=P))
@@ -48,6 +48,8 @@ def tile_tokenizer_kernel(tc, gene_embed, expr, w1, b1, w2, b2, bin0, bins, offs
             nc.sync.dma_start(x_all[:, tokens], expr[0:1, tokens].broadcast_to([P, LOAD]))
         window0 = held.tile([P, S], FP32, name="window0")
         nc.sync.dma_start(window0[:], gene_embed[0:P, :])
+        for tile, source in ((b2_sb, b2), (bins_sb, bins)):
+            nc.sync.dma_start(tile[:], source)
 
         identity = held.tile([P, P], FP32, name="identity")
         make_identity(nc, identity[:])

@@ -19,6 +19,8 @@ GROUPS = PIECE // P
 BANK_GROUPS = PIECE // E
 LOAD = 1024
 PSUM_BANKS = 8
+HALF = N // 2
+HALF_PIECES = HALF // PIECE
 
 FLOPS = 2 * N * (H * K + K * E)
 
@@ -63,7 +65,7 @@ def tile_tokenizer_kernel(tc, gene_embed, expr, w1, b1, w2, b2, bin0, bins, offs
         nc.vector.tensor_scalar_mul(w2_neg[:], w2_sb[:], -1.0)
 
         zero_bin = [held.tile([P, N], FP32, name=f"zero_bin{eb}") for eb in range(E_BLOCKS)]
-        t_all = [held.tile([P, N], FP32, name=f"t_all{eb}") for eb in range(E_BLOCKS)]
+        t_first = held.tile([P, N], FP32, name="t_first")
         hid_pos = held.tile([H, N], BF16, name="hid_pos")
         hid_neg = held.tile([H, N], BF16, name="hid_neg")
         expo = held.tile([K, N], BF16, name="expo")
@@ -72,9 +74,6 @@ def tile_tokenizer_kernel(tc, gene_embed, expr, w1, b1, w2, b2, bin0, bins, offs
         scale_col = held.tile([P, N // P], FP32, name="scale_col")
         q_tok = held.tile([P, N // P, E], FP32, name="q_tok")
         result = [held.tile([P, N], FP32, name=f"result{eb}") for eb in range(E_BLOCKS)]
-
-        def look_up(eb, window):
-            nc.vector.tensor_tensor(t_all[eb][:], window[:].indirect(offsets[:]), zero_bin[eb][:], ALU.add)
 
         for c in range(N // LOAD):
             tokens = slice(c * LOAD, (c + 1) * LOAD)
@@ -89,7 +88,7 @@ def tile_tokenizer_kernel(tc, gene_embed, expr, w1, b1, w2, b2, bin0, bins, offs
         window1 = shared.tile([P, S], FP32, name="window1", tag="expr_then_window")
         nc.sync.dma_start(window1[:], gene_embed[P : 2 * P, :])
 
-        look_up(0, window0)
+        nc.vector.tensor_tensor(t_first[:], window0[:].indirect(offsets[:]), zero_bin[0][:], ALU.add)
         with tc.psum_pool(name="psum_logit", bufs=4) as psum_logit, tc.psum_pool(name="psum_cols", bufs=1) as psum_cols:
             x_col = psum_cols.tile([P, P], FP32, name="x_col")
             nc.tensor.transpose(x_col[:], x_rows[:], identity[:])
@@ -106,23 +105,29 @@ def tile_tokenizer_kernel(tc, gene_embed, expr, w1, b1, w2, b2, bin0, bins, offs
             nc.vector.reciprocal(inv_col[:], sum_col[:])
             nc.vector.tensor_tensor(scale_col[:], inv_col[:], m_col[:], ALU.mult)
 
-        look_up(1, window1)
+        ring = ctx.enter_context(tc.tile_pool(name="ring", bufs=1))
         psum_late = ctx.enter_context(tc.psum_pool(name="psum_late", bufs=PSUM_BANKS))
-        for first in range(0, N // P, BANK_GROUPS):
-            mix_tok = psum_late.tile([P, BANK_GROUPS, E], FP32, name="mix_tok", tag="bank")
-            for a in range(BANK_GROUPS):
-                g = first + a
-                nc.tensor.matmul(mix_tok[:, a, :], expo[:, g * P : (g + 1) * P], bins_sb[:], start=True, stop=True)
-            for a in range(BANK_GROUPS):
-                g = first + a
-                nc.scalar.activation(q_tok[:, g, :], mix_tok[:, a, :], ACT.Copy, scale=scale_col[:, g : g + 1])
-
-        for i in range(PIECES):
-            cols = slice(i * PIECE, (i + 1) * PIECE)
-            for eb in range(E_BLOCKS):
-                mixed = psum_late.tile([P, PIECE], FP32, name="mixed", tag="bank")
-                for a in range(GROUPS):
-                    g = i * GROUPS + a
-                    nc.tensor.transpose(mixed[:, a * P : (a + 1) * P], q_tok[:, g, eb * P : (eb + 1) * P], identity[:])
-                nc.vector.tensor_tensor(result[eb][:, cols], t_all[eb][:, cols], mixed[:], ALU.add)
-                nc.sync.dma_start(out[eb * P : (eb + 1) * P, cols], result[eb][:, cols])
+        for half in range(N // HALF):
+            tokens = slice(half * HALF, (half + 1) * HALF)
+            pieces = range(half * HALF_PIECES, (half + 1) * HALF_PIECES)
+            t_second = ring.tile([P, HALF], FP32, name="t_second")
+            picked = window1[:].indirect(offsets[:, half * (HALF // 16) : (half + 1) * (HALF // 16)])
+            nc.vector.tensor_tensor(t_second[:], picked, zero_bin[1][:, tokens], ALU.add)
+            for first in range(pieces.start * GROUPS, pieces.stop * GROUPS, BANK_GROUPS):
+                mix_tok = psum_late.tile([P, BANK_GROUPS, E], FP32, name="mix_tok", tag="bank")
+                for a in range(BANK_GROUPS):
+                    g = first + a
+                    nc.tensor.matmul(mix_tok[:, a, :], expo[:, g * P : (g + 1) * P], bins_sb[:], start=True, stop=True)
+                for a in range(BANK_GROUPS):
+                    g = first + a
+                    nc.scalar.activation(q_tok[:, g, :], mix_tok[:, a, :], ACT.Copy, scale=scale_col[:, g : g + 1])
+            for i in pieces:
+                cols = slice(i * PIECE, (i + 1) * PIECE)
+                local = slice(cols.start - tokens.start, cols.stop - tokens.start)
+                for eb, t in ((0, t_first[:, cols]), (1, t_second[:, local])):
+                    mixed = psum_late.tile([P, PIECE], FP32, name="mixed", tag="bank")
+                    for a in range(GROUPS):
+                        g = i * GROUPS + a
+                        nc.tensor.transpose(mixed[:, a * P : (a + 1) * P], q_tok[:, g, eb * P : (eb + 1) * P], identity[:])
+                    nc.vector.tensor_tensor(result[eb][:, cols], t, mixed[:], ALU.add)
+                    nc.sync.dma_start(out[eb * P : (eb + 1) * P, cols], result[eb][:, cols])

@@ -47,7 +47,7 @@ def tile_tokenizer_kernel(tc, gene_embed, expr, w1, b1, w2, b2, bin0, bins, offs
         x_all = shared.tile([P, N], FP32, name="x_all", tag="expr_then_window")
         for c in range(N // LOAD):
             tokens = slice(c * LOAD, (c + 1) * LOAD)
-            nc.sync.dma_start(x_all[:, tokens], expr[0:1, tokens].broadcast_to([P, LOAD]))
+            nc.scalar.dma_start(x_all[:, tokens], expr[0:1, tokens].broadcast_to([P, LOAD]))
         window0 = held.tile([P, S], FP32, name="window0")
         nc.sync.dma_start(window0[:], gene_embed[0:P, :])
         for tile, source in ((b2_sb, b2), (bins_sb, bins)):

@@ -21,6 +21,7 @@ LOAD = 1024
 PSUM_BANKS = 8
 HALF = N // 2
 HALF_PIECES = HALF // PIECE
+LAST_HALF = N // HALF - 1
 
 FLOPS = 2 * N * (H * K + K * E)
 
@@ -125,9 +126,22 @@ def tile_tokenizer_kernel(tc, gene_embed, expr, w1, b1, w2, b2, bin0, bins, offs
                 cols = slice(i * PIECE, (i + 1) * PIECE)
                 local = slice(cols.start - tokens.start, cols.stop - tokens.start)
                 for eb, t in ((0, t_first[:, cols]), (1, t_second[:, local])):
+                    tensor_adds = eb == 0 and half == LAST_HALF
                     mixed = psum_late.tile([P, PIECE], FP32, name="mixed", tag="bank")
+                    if tensor_adds:
+                        nc.tensor.matmul(mixed[:], identity[:], t, start=True, stop=False)
                     for a in range(GROUPS):
                         g = i * GROUPS + a
-                        nc.tensor.transpose(mixed[:, a * P : (a + 1) * P], q_tok[:, g, eb * P : (eb + 1) * P], identity[:])
-                    nc.vector.tensor_tensor(result[eb][:, cols], t, mixed[:], ALU.add)
+                        nc.tensor.matmul(
+                            mixed[:, a * P : (a + 1) * P],
+                            q_tok[:, g, eb * P : (eb + 1) * P],
+                            identity[:],
+                            is_transpose=True,
+                            start=not tensor_adds,
+                            stop=not tensor_adds or a == GROUPS - 1,
+                        )
+                    if tensor_adds:
+                        nc.scalar.copy(result[eb][:, cols], mixed[:])
+                    else:
+                        nc.vector.tensor_tensor(result[eb][:, cols], t, mixed[:], ALU.add)
                     nc.sync.dma_start(out[eb * P : (eb + 1) * P, cols], result[eb][:, cols])

@@ -122,26 +122,29 @@ def tile_tokenizer_kernel(tc, gene_embed, expr, w1, b1, w2, b2, bin0, bins, offs
                 for a in range(BANK_GROUPS):
                     g = first + a
                     nc.scalar.activation(q_tok[:, g, :], mix_tok[:, a, :], ACT.Copy, scale=scale_col[:, g : g + 1])
-            for i in pieces:
+            if half == LAST_HALF:
+                order = [(i, eb) for eb in range(E_BLOCKS) for i in pieces]
+            else:
+                order = [(i, eb) for i in pieces for eb in range(E_BLOCKS)]
+            for i, eb in order:
                 cols = slice(i * PIECE, (i + 1) * PIECE)
-                local = slice(cols.start - tokens.start, cols.stop - tokens.start)
-                for eb, t in ((0, t_first[:, cols]), (1, t_second[:, local])):
-                    tensor_adds = eb == 0 and half == LAST_HALF
-                    mixed = psum_late.tile([P, PIECE], FP32, name="mixed", tag="bank")
-                    if tensor_adds:
-                        nc.tensor.matmul(mixed[:], identity[:], t, start=True, stop=False)
-                    for a in range(GROUPS):
-                        g = i * GROUPS + a
-                        nc.tensor.matmul(
-                            mixed[:, a * P : (a + 1) * P],
-                            q_tok[:, g, eb * P : (eb + 1) * P],
-                            identity[:],
-                            is_transpose=True,
-                            start=not tensor_adds,
-                            stop=not tensor_adds or a == GROUPS - 1,
-                        )
-                    if tensor_adds:
-                        nc.scalar.copy(result[eb][:, cols], mixed[:])
-                    else:
-                        nc.vector.tensor_tensor(result[eb][:, cols], t, mixed[:], ALU.add)
-                    nc.sync.dma_start(out[eb * P : (eb + 1) * P, cols], result[eb][:, cols])
+                t = t_first[:, cols] if eb == 0 else t_second[:, cols.start - tokens.start : cols.stop - tokens.start]
+                tensor_adds = eb == 0 and half == LAST_HALF
+                mixed = psum_late.tile([P, PIECE], FP32, name="mixed", tag="bank")
+                if tensor_adds:
+                    nc.tensor.matmul(mixed[:], identity[:], t, start=True, stop=False)
+                for a in range(GROUPS):
+                    g = i * GROUPS + a
+                    nc.tensor.matmul(
+                        mixed[:, a * P : (a + 1) * P],
+                        q_tok[:, g, eb * P : (eb + 1) * P],
+                        identity[:],
+                        is_transpose=True,
+                        start=not tensor_adds,
+                        stop=not tensor_adds or a == GROUPS - 1,
+                    )
+                if tensor_adds:
+                    nc.scalar.copy(result[eb][:, cols], mixed[:])
+                else:
+                    nc.vector.tensor_tensor(result[eb][:, cols], t, mixed[:], ALU.add)
+                nc.sync.dma_start(out[eb * P : (eb + 1) * P, cols], result[eb][:, cols])

@@ -145,6 +145,7 @@ def tile_tokenizer_kernel(tc, gene_embed, expr, w1, b1, w2, b2, bin0, bins, offs
                     )
                 if tensor_adds:
                     nc.scalar.copy(result[eb][:, cols], mixed[:])
+                    nc.scalar.dma_start(out[eb * P : (eb + 1) * P, cols], result[eb][:, cols])
                 else:
                     nc.vector.tensor_tensor(result[eb][:, cols], t, mixed[:], ALU.add)
-                nc.sync.dma_start(out[eb * P : (eb + 1) * P, cols], result[eb][:, cols])
+                    nc.sync.dma_start(out[eb * P : (eb + 1) * P, cols], result[eb][:, cols])

@@ -12,16 +12,18 @@ ACT = mybir.ActivationFunctionType
 P = 128
 E, S, N, H, K = 256, 4096, 4096, 128, 128
 SLOPE = 0.01
+ROWS = N // P
+PARTS = 3
 E_BLOCKS = E // P
 PIECE = 512
 PIECES = N // PIECE
 GROUPS = PIECE // P
 BANK_GROUPS = PIECE // E
-LOAD = 1024
 PSUM_BANKS = 8
-HALF = N // 2
-HALF_PIECES = HALF // PIECE
-LAST_HALF = N // HALF - 1
+SUM_BANKS = 2
+QUARTER = N // 4
+QUARTER_PIECES = QUARTER // PIECE
+LAST_QUARTER = N // QUARTER - 1
 
 FLOPS = 2 * N * (H * K + K * E)
 
@@ -30,34 +32,49 @@ def tile_tokenizer_kernel(tc, gene_embed, expr, w1, b1, w2, b2, bin0, bins, offs
     nc = tc.nc
     with ExitStack() as ctx:
         held = ctx.enter_context(tc.tile_pool(name="held", bufs=1))
-        shared = ctx.enter_context(tc.tile_pool(name="shared", bufs=1))
-        offsets = held.tile([P, N // 16], U16, name="offsets")
-        nc.sync.dma_start(offsets[:], offs)
+        turns = ctx.enter_context(tc.tile_pool(name="turns", bufs=1))
+        psum = ctx.enter_context(tc.psum_pool(name="psum", bufs=PSUM_BANKS - SUM_BANKS))
+        psum_sums = ctx.enter_context(tc.psum_pool(name="psum_sums", bufs=SUM_BANKS))
+
+        x_rows = held.tile([P, P], FP32, name="x_rows")
+        nc.vector.memset(x_rows[PARTS * ROWS : P, :], 0.0)
+        for part in range(PARTS):
+            nc.sync.dma_start(x_rows[part * ROWS : (part + 1) * ROWS, :], expr.rearrange("o (g r) -> (o g) r", r=P))
+        bin0_sb = held.tile([P, E_BLOCKS], FP32, name="bin0_sb")
         w1_sb = held.tile([P, 1], FP32, name="w1_sb")
         b1_sb = held.tile([P, 1], FP32, name="b1_sb")
         b2_sb = held.tile([P, 1], FP32, name="b2_sb")
         w2_sb = held.tile([H, K], BF16, name="w2_sb")
         bins_sb = held.tile([K, E], BF16, name="bins_sb")
-        for tile, source in ((w1_sb, w1), (b1_sb, b1), (w2_sb, w2)):
-            nc.sync.dma_start(tile[:], source)
-        bin0_sb = held.tile([P, E_BLOCKS], FP32, name="bin0_sb")
-        nc.sync.dma_start(bin0_sb[:], bin0.rearrange("(eb p) o -> p (eb o)", p=P))
-        x_rows = held.tile([P, P], FP32, name="x_rows")
-        nc.vector.memset(x_rows[:], 0.0)
-        nc.sync.dma_start(x_rows[0 : N // P, :], expr.rearrange("o (g r) -> (o g) r", r=P))
-        x_all = shared.tile([P, N], FP32, name="x_all", tag="expr_then_window")
-        for c in range(N // LOAD):
-            tokens = slice(c * LOAD, (c + 1) * LOAD)
-            nc.scalar.dma_start(x_all[:, tokens], expr[0:1, tokens].broadcast_to([P, LOAD]))
+        offsets = held.tile([P, N // 16], U16, name="offsets")
         window0 = held.tile([P, S], FP32, name="window0")
-        nc.sync.dma_start(window0[:], gene_embed[0:P, :])
-        for tile, source in ((b2_sb, b2), (bins_sb, bins)):
-            nc.sync.dma_start(tile[:], source)
+        x_all = held.tile([P, N], FP32, name="x_all")
+        window1 = held.tile([P, S], FP32, name="window1")
+        for tile, source in (
+            (w1_sb[:], w1),
+            (b1_sb[:], b1),
+            (w2_sb[:], w2),
+            (bin0_sb[:], bin0.rearrange("(eb p) o -> p (eb o)", p=P)),
+            (x_all[:, 0:QUARTER], expr[:, 0:QUARTER].broadcast_to([P, QUARTER])),
+            (window0[:], gene_embed[0:P, :]),
+            (offsets[:], offs),
+            (b2_sb[:], b2),
+            (x_all[:, QUARTER:N], expr[:, QUARTER:N].broadcast_to([P, N - QUARTER])),
+            (bins_sb[:], bins),
+            (window1[:], gene_embed[P : 2 * P, :]),
+        ):
+            nc.sync.dma_start(tile, source)
 
         identity = held.tile([P, P], FP32, name="identity")
         make_identity(nc, identity[:])
+        zero = held.tile([K, 1], FP32, name="zero")
+        nc.vector.memset(zero[:], 0.0)
         ones = held.tile([K, 1], BF16, name="ones")
-        nc.vector.memset(ones[:], 1.0)
+        nc.scalar.activation(ones[:], zero[:], ACT.Exp)
+        pick = held.tile([P, ROWS], BF16, name="pick")
+        pick_two = held.tile([P, ROWS], FP32, name="pick_two")
+        nc.gpsimd.tensor_tensor(pick_two[:], identity[:, 0:ROWS], identity[:, ROWS : 2 * ROWS], ALU.add)
+        nc.gpsimd.tensor_tensor(pick[:], pick_two[:], identity[:, 2 * ROWS : 3 * ROWS], ALU.add)
         w1_neg = held.tile([P, 1], FP32, name="w1_neg")
         b1_neg = held.tile([P, 1], FP32, name="b1_neg")
         w2_neg = held.tile([H, K], BF16, name="w2_neg")
@@ -65,87 +82,101 @@ def tile_tokenizer_kernel(tc, gene_embed, expr, w1, b1, w2, b2, bin0, bins, offs
         nc.vector.tensor_scalar_mul(b1_neg[:], b1_sb[:], -SLOPE)
         nc.vector.tensor_scalar_mul(w2_neg[:], w2_sb[:], -1.0)
 
-        zero_bin = [held.tile([P, N], FP32, name=f"zero_bin{eb}") for eb in range(E_BLOCKS)]
+        zero_bin_first = held.tile([P, N], FP32, name="zero_bin_first")
         t_first = held.tile([P, N], FP32, name="t_first")
         hid_pos = held.tile([H, N], BF16, name="hid_pos")
         hid_neg = held.tile([H, N], BF16, name="hid_neg")
         expo = held.tile([K, N], BF16, name="expo")
-        m_col = held.tile([P, N // P], FP32, name="m_col")
-        inv_col = held.tile([P, N // P], FP32, name="inv_col")
-        scale_col = held.tile([P, N // P], FP32, name="scale_col")
+        m_col = held.tile([P, ROWS], FP32, name="m_col")
+        scale_col = held.tile([P, ROWS], FP32, name="scale_col")
         q_tok = held.tile([P, N // P, E], FP32, name="q_tok")
         result = [held.tile([P, N], FP32, name=f"result{eb}") for eb in range(E_BLOCKS)]
 
-        for c in range(N // LOAD):
-            tokens = slice(c * LOAD, (c + 1) * LOAD)
-            for eb in range(E_BLOCKS):
-                nc.vector.tensor_scalar(
-                    zero_bin[eb][:, tokens], x_all[:, tokens], 0.0, bin0_sb[:, eb : eb + 1], ALU.is_equal, ALU.mult
-                )
+        x_parts = held.tile([P, P], BF16, name="x_parts")
+        x_rest = held.tile([P, P], FP32, name="x_rest")
+        x_mid = held.tile([P, P], BF16, name="x_mid")
+        mid = slice(ROWS, 2 * ROWS)
+        last = slice(2 * ROWS, 3 * ROWS)
+        nc.vector.tensor_copy(x_parts[:], x_rows[:])
+        nc.vector.tensor_tensor(x_rest[:], x_rows[:], x_parts[:], ALU.subtract)
+        nc.vector.tensor_copy(x_parts[mid, :], x_rest[mid, :])
+        nc.vector.tensor_copy(x_mid[last, :], x_rest[last, :])
+        nc.vector.tensor_tensor(x_parts[last, :], x_rest[last, :], x_mid[last, :], ALU.subtract)
+        nc.vector.tensor_scalar(zero_bin_first[:, 0:QUARTER], x_all[:, 0:QUARTER], 0.0, bin0_sb[:, 0:1], ALU.is_equal, ALU.mult)
         for i in range(PIECES):
             cols = slice(i * PIECE, (i + 1) * PIECE)
-            nc.scalar.activation(hid_pos[:, cols], x_all[:, cols], ACT.Relu, bias=b1_sb[:], scale=w1_sb[:])
-            nc.scalar.activation(hid_neg[:, cols], x_all[:, cols], ACT.Relu, bias=b1_neg[:], scale=w1_neg[:])
-        window1 = shared.tile([P, S], FP32, name="window1", tag="expr_then_window")
-        nc.sync.dma_start(window1[:], gene_embed[P : 2 * P, :])
+            x_piece = x_all[:, cols]
+            if i >= QUARTER_PIECES:
+                spread = psum.tile([P, PIECE], FP32, name="spread", tag="bank")
+                x_piece = spread[:]
+                for a in range(GROUPS):
+                    g = i * GROUPS + a
+                    nc.tensor.matmul(
+                        spread[:, a * P : (a + 1) * P], pick[:, g : g + 1].to_broadcast([P, P]), x_parts[:], start=True, stop=True
+                    )
+                nc.vector.tensor_scalar(zero_bin_first[:, cols], x_piece, 0.0, bin0_sb[:, 0:1], ALU.is_equal, ALU.mult)
+            nc.scalar.activation(hid_pos[:, cols], x_piece, ACT.Relu, bias=b1_sb[:], scale=w1_sb[:])
+            nc.scalar.activation(hid_neg[:, cols], x_piece, ACT.Relu, bias=b1_neg[:], scale=w1_neg[:])
+        x_col = psum.tile([P, P], FP32, name="x_col", tag="bank")
+        nc.tensor.transpose(x_col[:], x_rows[:], identity[:])
+        nc.vector.tensor_single_scalar(m_col[:], x_col[:, 0:ROWS], 0.0, ALU.not_equal)
 
-        nc.vector.tensor_tensor(t_first[:], window0[:].indirect(offsets[:]), zero_bin[0][:], ALU.add)
-        with tc.psum_pool(name="psum_logit", bufs=4) as psum_logit, tc.psum_pool(name="psum_cols", bufs=1) as psum_cols:
-            x_col = psum_cols.tile([P, P], FP32, name="x_col")
-            nc.tensor.transpose(x_col[:], x_rows[:], identity[:])
-            nc.vector.tensor_single_scalar(m_col[:], x_col[:, 0 : N // P], 0.0, ALU.not_equal)
-            sum_col = psum_cols.tile([P, N // P], FP32, name="sum_col")
-            for i in range(PIECES):
-                cols = slice(i * PIECE, (i + 1) * PIECE)
-                logit = psum_logit.tile([K, PIECE], FP32, name="logit")
-                nc.tensor.matmul(logit[:], w2_sb[:], hid_pos[:, cols], start=True, stop=False)
-                nc.tensor.matmul(logit[:], w2_neg[:], hid_neg[:, cols], start=False, stop=True)
-                nc.scalar.activation(expo[:, cols], logit[:], ACT.Exp, bias=b2_sb[:], scale=1.0)
-                for g in range(i * GROUPS, (i + 1) * GROUPS):
-                    nc.tensor.matmul(sum_col[:, g : g + 1], expo[:, g * P : (g + 1) * P], ones[:], start=True, stop=True)
-            nc.vector.reciprocal(inv_col[:], sum_col[:])
-            nc.vector.tensor_tensor(scale_col[:], inv_col[:], m_col[:], ALU.mult)
+        nc.vector.tensor_tensor(t_first[:], window0[:].indirect(offsets[:]), zero_bin_first[:], ALU.add)
+        sum_col = [psum_sums.tile([P, ROWS // SUM_BANKS], FP32, name=f"sum_col{h}", tag="sums") for h in range(SUM_BANKS)]
+        for i in range(PIECES):
+            cols = slice(i * PIECE, (i + 1) * PIECE)
+            logit = psum.tile([K, PIECE], FP32, name="logit", tag="bank")
+            nc.tensor.matmul(logit[:], w2_sb[:], hid_pos[:, cols], start=True, stop=False)
+            nc.tensor.matmul(logit[:], w2_neg[:], hid_neg[:, cols], start=False, stop=True)
+            nc.scalar.activation(expo[:, cols], logit[:], ACT.Exp, bias=b2_sb[:], scale=1.0)
+            for g in range(i * GROUPS, (i + 1) * GROUPS):
+                k, h = divmod(g, SUM_BANKS)
+                nc.tensor.matmul(sum_col[h][:, k : k + 1], expo[:, g * P : (g + 1) * P], ones[:], start=True, stop=True)
+        inv_col = turns.tile([P, ROWS], FP32, name="inv_col", tag="inv_then_t")
+        for h in range(SUM_BANKS):
+            nc.vector.reciprocal(inv_col[:, h::SUM_BANKS], sum_col[h][:])
+        nc.vector.tensor_tensor(scale_col[:], inv_col[:], m_col[:], ALU.mult)
 
-        ring = ctx.enter_context(tc.tile_pool(name="ring", bufs=1))
-        psum_late = ctx.enter_context(tc.psum_pool(name="psum_late", bufs=PSUM_BANKS))
-        for half in range(N // HALF):
-            tokens = slice(half * HALF, (half + 1) * HALF)
-            pieces = range(half * HALF_PIECES, (half + 1) * HALF_PIECES)
-            t_second = ring.tile([P, HALF], FP32, name="t_second")
-            picked = window1[:].indirect(offsets[:, half * (HALF // 16) : (half + 1) * (HALF // 16)])
-            nc.vector.tensor_tensor(t_second[:], picked, zero_bin[1][:, tokens], ALU.add)
+        for quarter in range(N // QUARTER):
+            tokens = slice(quarter * QUARTER, (quarter + 1) * QUARTER)
+            pieces = range(quarter * QUARTER_PIECES, (quarter + 1) * QUARTER_PIECES)
+            zero_bin_second = turns.tile([P, QUARTER], FP32, name="zero_bin_second")
+            nc.vector.tensor_scalar(zero_bin_second[:], x_all[:, tokens], 0.0, bin0_sb[:, 1:2], ALU.is_equal, ALU.mult)
+            t_second = turns.tile([P, QUARTER], FP32, name="t_second", tag="inv_then_t")
+            picked = window1[:].indirect(offsets[:, quarter * (QUARTER // 16) : (quarter + 1) * (QUARTER // 16)])
+            nc.vector.tensor_tensor(t_second[:], picked, zero_bin_second[:], ALU.add)
             for first in range(pieces.start * GROUPS, pieces.stop * GROUPS, BANK_GROUPS):
-                mix_tok = psum_late.tile([P, BANK_GROUPS, E], FP32, name="mix_tok", tag="bank")
+                mix_tok = psum.tile([P, BANK_GROUPS, E], FP32, name="mix_tok", tag="bank")
                 for a in range(BANK_GROUPS):
                     g = first + a
                     nc.tensor.matmul(mix_tok[:, a, :], expo[:, g * P : (g + 1) * P], bins_sb[:], start=True, stop=True)
                 for a in range(BANK_GROUPS):
                     g = first + a
                     nc.scalar.activation(q_tok[:, g, :], mix_tok[:, a, :], ACT.Copy, scale=scale_col[:, g : g + 1])
-            if half == LAST_HALF:
-                order = [(i, eb) for eb in range(E_BLOCKS) for i in pieces]
-            else:
-                order = [(i, eb) for i in pieces for eb in range(E_BLOCKS)]
-            for i, eb in order:
+            for i in pieces:
                 cols = slice(i * PIECE, (i + 1) * PIECE)
-                t = t_first[:, cols] if eb == 0 else t_second[:, cols.start - tokens.start : cols.stop - tokens.start]
-                tensor_adds = eb == 0 and half == LAST_HALF
-                mixed = psum_late.tile([P, PIECE], FP32, name="mixed", tag="bank")
-                if tensor_adds:
-                    nc.tensor.matmul(mixed[:], identity[:], t, start=True, stop=False)
-                for a in range(GROUPS):
-                    g = i * GROUPS + a
-                    nc.tensor.matmul(
-                        mixed[:, a * P : (a + 1) * P],
-                        q_tok[:, g, eb * P : (eb + 1) * P],
-                        identity[:],
-                        is_transpose=True,
-                        start=not tensor_adds,
-                        stop=not tensor_adds or a == GROUPS - 1,
-                    )
-                if tensor_adds:
-                    nc.scalar.copy(result[eb][:, cols], mixed[:])
-                    nc.scalar.dma_start(out[eb * P : (eb + 1) * P, cols], result[eb][:, cols])
-                else:
-                    nc.vector.tensor_tensor(result[eb][:, cols], t, mixed[:], ALU.add)
-                    nc.sync.dma_start(out[eb * P : (eb + 1) * P, cols], result[eb][:, cols])
+                for eb in range(E_BLOCKS):
+                    t = t_first[:, cols] if eb == 0 else t_second[:, cols.start - tokens.start : cols.stop - tokens.start]
+                    tensor_adds = eb == 0 and quarter < LAST_QUARTER
+                    if tensor_adds:
+                        mixed = psum_sums.tile([P, PIECE], FP32, name="mixed", tag="sums")
+                    else:
+                        mixed = psum.tile([P, PIECE], FP32, name="mixed", tag="bank")
+                    if tensor_adds:
+                        nc.tensor.matmul(mixed[:], identity[:], t, start=True, stop=False)
+                    for a in range(GROUPS):
+                        g = i * GROUPS + a
+                        nc.tensor.matmul(
+                            mixed[:, a * P : (a + 1) * P],
+                            q_tok[:, g, eb * P : (eb + 1) * P],
+                            identity[:],
+                            is_transpose=True,
+                            start=not tensor_adds,
+                            stop=not tensor_adds or a == GROUPS - 1,
+                        )
+                    if tensor_adds:
+                        nc.scalar.copy(result[eb][:, cols], mixed[:])
+                        nc.scalar.dma_start(out[eb * P : (eb + 1) * P, cols], result[eb][:, cols])
+                    else:
+                        nc.vector.tensor_tensor(result[eb][:, cols], t, mixed[:], ALU.add)
+                        nc.sync.dma_start(out[eb * P : (eb + 1) * P, cols], result[eb][:, cols])

@@ -23,7 +23,6 @@ PSUM_BANKS = 8
 SUM_BANKS = 2
 QUARTER = N // 4
 QUARTER_PIECES = QUARTER // PIECE
-LAST_QUARTER = N // QUARTER - 1
 
 FLOPS = 2 * N * (H * K + K * E)
 
@@ -157,7 +156,7 @@ def tile_tokenizer_kernel(tc, gene_embed, expr, w1, b1, w2, b2, bin0, bins, offs
                 cols = slice(i * PIECE, (i + 1) * PIECE)
                 for eb in range(E_BLOCKS):
                     t = t_first[:, cols] if eb == 0 else t_second[:, cols.start - tokens.start : cols.stop - tokens.start]
-                    tensor_adds = eb == 0 and quarter < LAST_QUARTER
+                    tensor_adds = eb == 0
                     if tensor_adds:
                         mixed = psum_sums.tile([P, PIECE], FP32, name="mixed", tag="sums")
                     else:

@@ -31,11 +31,13 @@ def tile_tokenizer_kernel(tc, gene_embed, expr, w1, b1, w2, b2, bin0, bins, offs
     nc = tc.nc
     with ExitStack() as ctx:
         held = ctx.enter_context(tc.tile_pool(name="held", bufs=1))
-        turns = ctx.enter_context(tc.tile_pool(name="turns", bufs=1))
+        turns = ctx.enter_context(tc.tile_pool(name="turns", bufs=2))
         psum = ctx.enter_context(tc.psum_pool(name="psum", bufs=PSUM_BANKS - SUM_BANKS))
         psum_sums = ctx.enter_context(tc.psum_pool(name="psum_sums", bufs=SUM_BANKS))
 
         x_rows = held.tile([P, P], FP32, name="x_rows")
+        not_m_rows = held.tile([ROWS, P], FP32, name="not_m_rows")
+        parked = out[0:1, :]
         nc.vector.memset(x_rows[PARTS * ROWS : P, :], 0.0)
         for part in range(PARTS):
             nc.sync.dma_start(x_rows[part * ROWS : (part + 1) * ROWS, :], expr.rearrange("o (g r) -> (o g) r", r=P))
@@ -47,22 +49,25 @@ def tile_tokenizer_kernel(tc, gene_embed, expr, w1, b1, w2, b2, bin0, bins, offs
         bins_sb = held.tile([K, E], BF16, name="bins_sb")
         offsets = held.tile([P, N // 16], U16, name="offsets")
         window0 = held.tile([P, S], FP32, name="window0")
-        x_all = held.tile([P, N], FP32, name="x_all")
+        x_first = held.tile([P, QUARTER], FP32, name="x_first")
+        not_m_others = held.tile([P, N - QUARTER], FP32, name="not_m_others")
         window1 = held.tile([P, S], FP32, name="window1")
         for tile, source in (
             (w1_sb[:], w1),
             (b1_sb[:], b1),
             (w2_sb[:], w2),
             (bin0_sb[:], bin0.rearrange("(eb p) o -> p (eb o)", p=P)),
-            (x_all[:, 0:QUARTER], expr[:, 0:QUARTER].broadcast_to([P, QUARTER])),
+            (x_first[:], expr[:, 0:QUARTER].broadcast_to([P, QUARTER])),
             (window0[:], gene_embed[0:P, :]),
             (offsets[:], offs),
             (b2_sb[:], b2),
-            (x_all[:, QUARTER:N], expr[:, QUARTER:N].broadcast_to([P, N - QUARTER])),
             (bins_sb[:], bins),
-            (window1[:], gene_embed[P : 2 * P, :]),
         ):
             nc.sync.dma_start(tile, source)
+        nc.vector.tensor_single_scalar(not_m_rows[:], x_rows[0:ROWS, :], 0.0, ALU.is_equal)
+        nc.sync.dma_start(parked.rearrange("o (g r) -> (o g) r", r=P), not_m_rows[:])
+        nc.sync.dma_start(not_m_others[:], parked[:, QUARTER:N].broadcast_to([P, N - QUARTER]))
+        nc.sync.dma_start(window1[:], gene_embed[P : 2 * P, :])
 
         identity = held.tile([P, P], FP32, name="identity")
         make_identity(nc, identity[:])
@@ -82,12 +87,12 @@ def tile_tokenizer_kernel(tc, gene_embed, expr, w1, b1, w2, b2, bin0, bins, offs
         nc.vector.tensor_scalar_mul(w2_neg[:], w2_sb[:], -1.0)
 
         zero_bin_first = held.tile([P, N], FP32, name="zero_bin_first")
+        zero_bin_second = held.tile([P, N], FP32, name="zero_bin_second")
         t_first = held.tile([P, N], FP32, name="t_first")
         hid_pos = held.tile([H, N], BF16, name="hid_pos")
         hid_neg = held.tile([H, N], BF16, name="hid_neg")
         expo = held.tile([K, N], BF16, name="expo")
-        m_col = held.tile([P, ROWS], FP32, name="m_col")
-        scale_col = held.tile([P, ROWS], FP32, name="scale_col")
+        scale_col = held.tile([P, SUM_BANKS, ROWS // SUM_BANKS], FP32, name="scale_col")
         q_tok = held.tile([P, N // P, E], FP32, name="q_tok")
         result = [held.tile([P, N], FP32, name=f"result{eb}") for eb in range(E_BLOCKS)]
 
@@ -101,11 +106,13 @@ def tile_tokenizer_kernel(tc, gene_embed, expr, w1, b1, w2, b2, bin0, bins, offs
         nc.vector.tensor_copy(x_parts[mid, :], x_rest[mid, :])
         nc.vector.tensor_copy(x_mid[last, :], x_rest[last, :])
         nc.vector.tensor_tensor(x_parts[last, :], x_rest[last, :], x_mid[last, :], ALU.subtract)
-        nc.vector.tensor_scalar(zero_bin_first[:, 0:QUARTER], x_all[:, 0:QUARTER], 0.0, bin0_sb[:, 0:1], ALU.is_equal, ALU.mult)
+        nc.vector.tensor_scalar(zero_bin_first[:, 0:QUARTER], x_first[:], 0.0, bin0_sb[:, 0:1], ALU.is_equal, ALU.mult)
+        nc.vector.tensor_scalar(zero_bin_second[:, 0:QUARTER], x_first[:], 0.0, bin0_sb[:, 1:2], ALU.is_equal, ALU.mult)
         for i in range(PIECES):
             cols = slice(i * PIECE, (i + 1) * PIECE)
-            x_piece = x_all[:, cols]
-            if i >= QUARTER_PIECES:
+            if i < QUARTER_PIECES:
+                x_piece = x_first[:, cols]
+            else:
                 spread = psum.tile([P, PIECE], FP32, name="spread", tag="bank")
                 x_piece = spread[:]
                 for a in range(GROUPS):
@@ -116,9 +123,15 @@ def tile_tokenizer_kernel(tc, gene_embed, expr, w1, b1, w2, b2, bin0, bins, offs
                 nc.vector.tensor_scalar(zero_bin_first[:, cols], x_piece, 0.0, bin0_sb[:, 0:1], ALU.is_equal, ALU.mult)
             nc.scalar.activation(hid_pos[:, cols], x_piece, ACT.Relu, bias=b1_sb[:], scale=w1_sb[:])
             nc.scalar.activation(hid_neg[:, cols], x_piece, ACT.Relu, bias=b1_neg[:], scale=w1_neg[:])
+        m_col = held.tile([P, ROWS], FP32, name="m_col")
         x_col = psum.tile([P, P], FP32, name="x_col", tag="bank")
         nc.tensor.transpose(x_col[:], x_rows[:], identity[:])
         nc.vector.tensor_single_scalar(m_col[:], x_col[:, 0:ROWS], 0.0, ALU.not_equal)
+
+        def scalar_zero_bin(quarter):
+            tokens = slice(quarter * QUARTER, (quarter + 1) * QUARTER)
+            not_m = not_m_others[:, tokens.start - QUARTER : tokens.stop - QUARTER]
+            nc.scalar.activation(zero_bin_second[:, tokens], not_m, ACT.Copy, scale=bin0_sb[:, 1:2])
 
         nc.vector.tensor_tensor(t_first[:], window0[:].indirect(offsets[:]), zero_bin_first[:], ALU.add)
         sum_col = [psum_sums.tile([P, ROWS // SUM_BANKS], FP32, name=f"sum_col{h}", tag="sums") for h in range(SUM_BANKS)]
@@ -131,19 +144,18 @@ def tile_tokenizer_kernel(tc, gene_embed, expr, w1, b1, w2, b2, bin0, bins, offs
             for g in range(i * GROUPS, (i + 1) * GROUPS):
                 k, h = divmod(g, SUM_BANKS)
                 nc.tensor.matmul(sum_col[h][:, k : k + 1], expo[:, g * P : (g + 1) * P], ones[:], start=True, stop=True)
-        inv_col = turns.tile([P, ROWS], FP32, name="inv_col", tag="inv_then_t")
+        scalar_zero_bin(1)
         for h in range(SUM_BANKS):
-            nc.vector.reciprocal(inv_col[:, h::SUM_BANKS], sum_col[h][:])
-        nc.vector.tensor_tensor(scale_col[:], inv_col[:], m_col[:], ALU.mult)
+            inv_col = turns.tile([P, ROWS // SUM_BANKS], FP32, name="inv_col", tag="inv_then_t")
+            nc.vector.reciprocal(inv_col[:], sum_col[h][:])
+            nc.vector.tensor_tensor(scale_col[:, h, :], inv_col[:], m_col[:, h::SUM_BANKS], ALU.mult)
 
         for quarter in range(N // QUARTER):
             tokens = slice(quarter * QUARTER, (quarter + 1) * QUARTER)
             pieces = range(quarter * QUARTER_PIECES, (quarter + 1) * QUARTER_PIECES)
-            zero_bin_second = turns.tile([P, QUARTER], FP32, name="zero_bin_second")
-            nc.vector.tensor_scalar(zero_bin_second[:], x_all[:, tokens], 0.0, bin0_sb[:, 1:2], ALU.is_equal, ALU.mult)
             t_second = turns.tile([P, QUARTER], FP32, name="t_second", tag="inv_then_t")
             picked = window1[:].indirect(offsets[:, quarter * (QUARTER // 16) : (quarter + 1) * (QUARTER // 16)])
-            nc.vector.tensor_tensor(t_second[:], picked, zero_bin_second[:], ALU.add)
+            nc.vector.tensor_tensor(t_second[:], picked, zero_bin_second[:, tokens], ALU.add)
             for first in range(pieces.start * GROUPS, pieces.stop * GROUPS, BANK_GROUPS):
                 mix_tok = psum.tile([P, BANK_GROUPS, E], FP32, name="mix_tok", tag="bank")
                 for a in range(BANK_GROUPS):
@@ -151,12 +163,14 @@ def tile_tokenizer_kernel(tc, gene_embed, expr, w1, b1, w2, b2, bin0, bins, offs
                     nc.tensor.matmul(mix_tok[:, a, :], expo[:, g * P : (g + 1) * P], bins_sb[:], start=True, stop=True)
                 for a in range(BANK_GROUPS):
                     g = first + a
-                    nc.scalar.activation(q_tok[:, g, :], mix_tok[:, a, :], ACT.Copy, scale=scale_col[:, g : g + 1])
+                    nc.scalar.activation(q_tok[:, g, :], mix_tok[:, a, :], ACT.Copy, scale=scale_col[:, g % SUM_BANKS, g // SUM_BANKS : g // SUM_BANKS + 1])
+            if quarter + 2 < N // QUARTER:
+                scalar_zero_bin(quarter + 2)
             for i in pieces:
                 cols = slice(i * PIECE, (i + 1) * PIECE)
                 for eb in range(E_BLOCKS):
                     t = t_first[:, cols] if eb == 0 else t_second[:, cols.start - tokens.start : cols.stop - tokens.start]
-                    tensor_adds = eb == 0
+                    tensor_adds = eb == 0 and i % 4 != 3
                     if tensor_adds:
                         mixed = psum_sums.tile([P, PIECE], FP32, name="mixed", tag="sums")
                     else:

@@ -170,7 +170,7 @@ def tile_tokenizer_kernel(tc, gene_embed, expr, w1, b1, w2, b2, bin0, bins, offs
                 cols = slice(i * PIECE, (i + 1) * PIECE)
                 for eb in range(E_BLOCKS):
                     t = t_first[:, cols] if eb == 0 else t_second[:, cols.start - tokens.start : cols.stop - tokens.start]
-                    tensor_adds = eb == 0 and i % 4 != 3
+                    tensor_adds = eb == 0 and i % 2 == 0
                     if tensor_adds:
                         mixed = psum_sums.tile([P, PIECE], FP32, name="mixed", tag="sums")
                     else:

@@ -55,11 +55,11 @@ def tile_tokenizer_kernel(tc, gene_embed, expr, w1, b1, w2, b2, bin0, bins, offs
         for tile, source in (
             (w1_sb[:], w1),
             (b1_sb[:], b1),
-            (w2_sb[:], w2),
             (bin0_sb[:], bin0.rearrange("(eb p) o -> p (eb o)", p=P)),
             (x_first[:], expr[:, 0:QUARTER].broadcast_to([P, QUARTER])),
             (window0[:], gene_embed[0:P, :]),
             (offsets[:], offs),
+            (w2_sb[:], w2),
             (b2_sb[:], b2),
             (bins_sb[:], bins),
         ):
@@ -84,7 +84,6 @@ def tile_tokenizer_kernel(tc, gene_embed, expr, w1, b1, w2, b2, bin0, bins, offs
         w2_neg = held.tile([H, K], BF16, name="w2_neg")
         nc.vector.tensor_scalar_mul(w1_neg[:], w1_sb[:], -SLOPE)
         nc.vector.tensor_scalar_mul(b1_neg[:], b1_sb[:], -SLOPE)
-        nc.vector.tensor_scalar_mul(w2_neg[:], w2_sb[:], -1.0)
 
         zero_bin_first = held.tile([P, N], FP32, name="zero_bin_first")
         zero_bin_second = held.tile([P, N], FP32, name="zero_bin_second")
@@ -123,6 +122,8 @@ def tile_tokenizer_kernel(tc, gene_embed, expr, w1, b1, w2, b2, bin0, bins, offs
                 nc.vector.tensor_scalar(zero_bin_first[:, cols], x_piece, 0.0, bin0_sb[:, 0:1], ALU.is_equal, ALU.mult)
             nc.scalar.activation(hid_pos[:, cols], x_piece, ACT.Relu, bias=b1_sb[:], scale=w1_sb[:])
             nc.scalar.activation(hid_neg[:, cols], x_piece, ACT.Relu, bias=b1_neg[:], scale=w1_neg[:])
+            if i == PIECES - QUARTER_PIECES - 1:
+                nc.scalar.mul(w2_neg[:], w2_sb[:], -1.0)
         m_col = held.tile([P, ROWS], FP32, name="m_col")
         x_col = psum.tile([P, P], FP32, name="x_col", tag="bank")
         nc.tensor.transpose(x_col[:], x_rows[:], identity[:])

from contextlib import ExitStack

import concourse.mybir as mybir
from concourse.masks import make_identity

FP32 = mybir.dt.float32
BF16 = mybir.dt.bfloat16
U16 = mybir.dt.uint16
ALU = mybir.AluOpType
ACT = mybir.ActivationFunctionType

P = 128
E, S, N, H, K = 256, 4096, 4096, 128, 128
SLOPE = 0.01
ROWS = N // P
PARTS = 3
E_BLOCKS = E // P
PIECE = 512
PIECES = N // PIECE
GROUPS = PIECE // P
BANK_GROUPS = PIECE // E
PSUM_BANKS = 8
SUM_BANKS = 2
QUARTER = N // 4
QUARTER_PIECES = QUARTER // PIECE

FLOPS = 2 * N * (H * K + K * E)


def tile_tokenizer_kernel(tc, gene_embed, expr, w1, b1, w2, b2, bin0, bins, offs, out):
    nc = tc.nc
    with ExitStack() as ctx:
        held = ctx.enter_context(tc.tile_pool(name="held", bufs=1))
        turns = ctx.enter_context(tc.tile_pool(name="turns", bufs=2))
        psum = ctx.enter_context(tc.psum_pool(name="psum", bufs=PSUM_BANKS - SUM_BANKS))
        psum_sums = ctx.enter_context(tc.psum_pool(name="psum_sums", bufs=SUM_BANKS))

        x_rows = held.tile([P, P], FP32, name="x_rows")
        not_m_rows = held.tile([ROWS, P], FP32, name="not_m_rows")
        parked = out[0:1, :]
        nc.vector.memset(x_rows[PARTS * ROWS : P, :], 0.0)
        for part in range(PARTS):
            nc.sync.dma_start(x_rows[part * ROWS : (part + 1) * ROWS, :], expr.rearrange("o (g r) -> (o g) r", r=P))
        bin0_sb = held.tile([P, E_BLOCKS], FP32, name="bin0_sb")
        w1_sb = held.tile([P, 1], FP32, name="w1_sb")
        b1_sb = held.tile([P, 1], FP32, name="b1_sb")
        b2_sb = held.tile([P, 1], FP32, name="b2_sb")
        w2_sb = held.tile([H, K], BF16, name="w2_sb")
        bins_sb = held.tile([K, E], BF16, name="bins_sb")
        offsets = held.tile([P, N // 16], U16, name="offsets")
        window0 = held.tile([P, S], FP32, name="window0")
        x_first = held.tile([P, QUARTER], FP32, name="x_first")
        not_m_others = held.tile([P, N - QUARTER], FP32, name="not_m_others")
        window1 = held.tile([P, S], FP32, name="window1")
        for tile, source in (
            (w1_sb[:], w1),
            (b1_sb[:], b1),
            (bin0_sb[:], bin0.rearrange("(eb p) o -> p (eb o)", p=P)),
            (x_first[:], expr[:, 0:QUARTER].broadcast_to([P, QUARTER])),
            (window0[:], gene_embed[0:P, :]),
            (offsets[:], offs),
            (w2_sb[:], w2),
            (b2_sb[:], b2),
            (bins_sb[:], bins),
        ):
            nc.sync.dma_start(tile, source)
        nc.vector.tensor_single_scalar(not_m_rows[:], x_rows[0:ROWS, :], 0.0, ALU.is_equal)
        nc.sync.dma_start(parked.rearrange("o (g r) -> (o g) r", r=P), not_m_rows[:])
        nc.sync.dma_start(not_m_others[:], parked[:, QUARTER:N].broadcast_to([P, N - QUARTER]))
        nc.sync.dma_start(window1[:], gene_embed[P : 2 * P, :])

        identity = held.tile([P, P], FP32, name="identity")
        make_identity(nc, identity[:])
        zero = held.tile([K, 1], FP32, name="zero")
        nc.vector.memset(zero[:], 0.0)
        ones = held.tile([K, 1], BF16, name="ones")
        nc.scalar.activation(ones[:], zero[:], ACT.Exp)
        pick = held.tile([P, ROWS], BF16, name="pick")
        pick_two = held.tile([P, ROWS], FP32, name="pick_two")
        nc.gpsimd.tensor_tensor(pick_two[:], identity[:, 0:ROWS], identity[:, ROWS : 2 * ROWS], ALU.add)
        nc.gpsimd.tensor_tensor(pick[:], pick_two[:], identity[:, 2 * ROWS : 3 * ROWS], ALU.add)
        w1_neg = held.tile([P, 1], FP32, name="w1_neg")
        b1_neg = held.tile([P, 1], FP32, name="b1_neg")
        w2_neg = held.tile([H, K], BF16, name="w2_neg")
        nc.vector.tensor_scalar_mul(w1_neg[:], w1_sb[:], -SLOPE)
        nc.vector.tensor_scalar_mul(b1_neg[:], b1_sb[:], -SLOPE)

        zero_bin_first = held.tile([P, N], FP32, name="zero_bin_first")
        zero_bin_second = held.tile([P, N], FP32, name="zero_bin_second")
        t_first = held.tile([P, N], FP32, name="t_first")
        hid_pos = held.tile([H, N], BF16, name="hid_pos")
        hid_neg = held.tile([H, N], BF16, name="hid_neg")
        expo = held.tile([K, N], BF16, name="expo")
        scale_col = held.tile([P, SUM_BANKS, ROWS // SUM_BANKS], FP32, name="scale_col")
        q_tok = held.tile([P, N // P, E], FP32, name="q_tok")
        result = [held.tile([P, N], FP32, name=f"result{eb}") for eb in range(E_BLOCKS)]

        x_parts = held.tile([P, P], BF16, name="x_parts")
        x_rest = held.tile([P, P], FP32, name="x_rest")
        x_mid = held.tile([P, P], BF16, name="x_mid")
        mid = slice(ROWS, 2 * ROWS)
        last = slice(2 * ROWS, 3 * ROWS)
        nc.vector.tensor_copy(x_parts[:], x_rows[:])
        nc.vector.tensor_tensor(x_rest[:], x_rows[:], x_parts[:], ALU.subtract)
        nc.vector.tensor_copy(x_parts[mid, :], x_rest[mid, :])
        nc.vector.tensor_copy(x_mid[last, :], x_rest[last, :])
        nc.vector.tensor_tensor(x_parts[last, :], x_rest[last, :], x_mid[last, :], ALU.subtract)
        nc.vector.tensor_scalar(zero_bin_first[:, 0:QUARTER], x_first[:], 0.0, bin0_sb[:, 0:1], ALU.is_equal, ALU.mult)
        nc.vector.tensor_scalar(zero_bin_second[:, 0:QUARTER], x_first[:], 0.0, bin0_sb[:, 1:2], ALU.is_equal, ALU.mult)
        for i in range(PIECES):
            cols = slice(i * PIECE, (i + 1) * PIECE)
            if i < QUARTER_PIECES:
                x_piece = x_first[:, cols]
            else:
                spread = psum.tile([P, PIECE], FP32, name="spread", tag="bank")
                x_piece = spread[:]
                for a in range(GROUPS):
                    g = i * GROUPS + a
                    nc.tensor.matmul(
                        spread[:, a * P : (a + 1) * P], pick[:, g : g + 1].to_broadcast([P, P]), x_parts[:], start=True, stop=True
                    )
                nc.vector.tensor_scalar(zero_bin_first[:, cols], x_piece, 0.0, bin0_sb[:, 0:1], ALU.is_equal, ALU.mult)
            nc.scalar.activation(hid_pos[:, cols], x_piece, ACT.Relu, bias=b1_sb[:], scale=w1_sb[:])
            nc.scalar.activation(hid_neg[:, cols], x_piece, ACT.Relu, bias=b1_neg[:], scale=w1_neg[:])
            if i == PIECES - QUARTER_PIECES - 1:
                nc.scalar.mul(w2_neg[:], w2_sb[:], -1.0)
        m_col = held.tile([P, ROWS], FP32, name="m_col")
        x_col = psum.tile([P, P], FP32, name="x_col", tag="bank")
        nc.tensor.transpose(x_col[:], x_rows[:], identity[:])
        nc.vector.tensor_single_scalar(m_col[:], x_col[:, 0:ROWS], 0.0, ALU.not_equal)

        def scalar_zero_bin(quarter):
            tokens = slice(quarter * QUARTER, (quarter + 1) * QUARTER)
            not_m = not_m_others[:, tokens.start - QUARTER : tokens.stop - QUARTER]
            nc.scalar.activation(zero_bin_second[:, tokens], not_m, ACT.Copy, scale=bin0_sb[:, 1:2])

        nc.vector.tensor_tensor(t_first[:], window0[:].indirect(offsets[:]), zero_bin_first[:], ALU.add)
        sum_col = [psum_sums.tile([P, ROWS // SUM_BANKS], FP32, name=f"sum_col{h}", tag="sums") for h in range(SUM_BANKS)]
        for i in range(PIECES):
            cols = slice(i * PIECE, (i + 1) * PIECE)
            logit = psum.tile([K, PIECE], FP32, name="logit", tag="bank")
            nc.tensor.matmul(logit[:], w2_sb[:], hid_pos[:, cols], start=True, stop=False)
            nc.tensor.matmul(logit[:], w2_neg[:], hid_neg[:, cols], start=False, stop=True)
            nc.scalar.activation(expo[:, cols], logit[:], ACT.Exp, bias=b2_sb[:], scale=1.0)
            for g in range(i * GROUPS, (i + 1) * GROUPS):
                k, h = divmod(g, SUM_BANKS)
                nc.tensor.matmul(sum_col[h][:, k : k + 1], expo[:, g * P : (g + 1) * P], ones[:], start=True, stop=True)
        scalar_zero_bin(1)
        for h in range(SUM_BANKS):
            inv_col = turns.tile([P, ROWS // SUM_BANKS], FP32, name="inv_col", tag="inv_then_t")
            nc.vector.reciprocal(inv_col[:], sum_col[h][:])
            nc.vector.tensor_tensor(scale_col[:, h, :], inv_col[:], m_col[:, h::SUM_BANKS], ALU.mult)

        for quarter in range(N // QUARTER):
            tokens = slice(quarter * QUARTER, (quarter + 1) * QUARTER)
            pieces = range(quarter * QUARTER_PIECES, (quarter + 1) * QUARTER_PIECES)
            t_second = turns.tile([P, QUARTER], FP32, name="t_second", tag="inv_then_t")
            picked = window1[:].indirect(offsets[:, quarter * (QUARTER // 16) : (quarter + 1) * (QUARTER // 16)])
            nc.vector.tensor_tensor(t_second[:], picked, zero_bin_second[:, tokens], ALU.add)
            for first in range(pieces.start * GROUPS, pieces.stop * GROUPS, BANK_GROUPS):
                mix_tok = psum.tile([P, BANK_GROUPS, E], FP32, name="mix_tok", tag="bank")
                for a in range(BANK_GROUPS):
                    g = first + a
                    nc.tensor.matmul(mix_tok[:, a, :], expo[:, g * P : (g + 1) * P], bins_sb[:], start=True, stop=True)
                for a in range(BANK_GROUPS):
                    g = first + a
                    nc.scalar.activation(q_tok[:, g, :], mix_tok[:, a, :], ACT.Copy, scale=scale_col[:, g % SUM_BANKS, g // SUM_BANKS : g // SUM_BANKS + 1])
            if quarter + 2 < N // QUARTER:
                scalar_zero_bin(quarter + 2)
            for i in pieces:
                cols = slice(i * PIECE, (i + 1) * PIECE)
                for eb in range(E_BLOCKS):
                    t = t_first[:, cols] if eb == 0 else t_second[:, cols.start - tokens.start : cols.stop - tokens.start]
                    tensor_adds = eb == 0 and i % 2 == 0
                    if tensor_adds:
                        mixed = psum_sums.tile([P, PIECE], FP32, name="mixed", tag="sums")
                    else:
                        mixed = psum.tile([P, PIECE], FP32, name="mixed", tag="bank")
                    if tensor_adds:
                        nc.tensor.matmul(mixed[:], identity[:], t, start=True, stop=False)
                    for a in range(GROUPS):
                        g = i * GROUPS + a
                        nc.tensor.matmul(
                            mixed[:, a * P : (a + 1) * P],
                            q_tok[:, g, eb * P : (eb + 1) * P],
                            identity[:],
                            is_transpose=True,
                            start=not tensor_adds,
                            stop=not tensor_adds or a == GROUPS - 1,
                        )
                    if tensor_adds:
                        nc.scalar.copy(result[eb][:, cols], mixed[:])
                        nc.scalar.dma_start(out[eb * P : (eb + 1) * P, cols], result[eb][:, cols])
                    else:
                        nc.vector.tensor_tensor(result[eb][:, cols], t, mixed[:], ALU.add)
                        nc.sync.dma_start(out[eb * P : (eb + 1) * P, cols], result[eb][:, cols])
